import numpy as np
import ml_dtypes

BF16 = ml_dtypes.bfloat16


def bf(x):
    return np.asarray(x, np.float32).astype(BF16)


def f32(x):
    return np.asarray(x, np.float32)


def f64(x):
    return np.asarray(x).astype(np.float64)


def striped(idx):
    return np.tile(idx.reshape(-1, 16).T, (8, 1))


C, S, N = 128, 512, 256
EPS = 1e-6
PE_BASE = 10000.0


def pos_table():
    pos = np.arange(N, dtype=np.float32)[:, None]
    div = np.exp(np.arange(C // 2, dtype=np.float32) * np.float32(-np.log(PE_BASE) / (C // 2 - 1)))
    return np.ascontiguousarray(np.concatenate([np.sin(pos * div), np.cos(pos * div)], axis=-1).T)


def setup_inputs():
    return {"emb": f32(np.random.standard_normal((C, S))), "pe": f32(pos_table()), "ln_w": f32(1.0 + 0.1 * np.random.standard_normal((C, 1))), "ln_b": f32(0.1 * np.random.standard_normal((C, 1))), "offs": striped(np.random.permutation(np.tile(np.arange(S), 2))[:N])}


def reference(emb, pe, ln_w, ln_b, offs):
    idx = offs[:16].T.reshape(-1)
    x = f64(emb)[:, idx] + f64(pe)
    m = x.mean(axis=0, keepdims=True)
    v = np.square(x - m).mean(axis=0, keepdims=True)
    h = (x - m) / np.sqrt(v + EPS) * f64(ln_w) + f64(ln_b)
    return np.concatenate([x, h], axis=0)

@@ -1,0 +1,66 @@
+import concourse.mybir as mybir
+
+F32 = mybir.dt.float32
+U16 = mybir.dt.uint16
+ALU = mybir.AluOpType
+ACT = mybir.ActivationFunctionType
+
+C, S, N = 128, 512, 256
+EPS = 1e-6
+FLOPS = 2 * 2 * C * C * N
+
+
+def tile_transformernet_kernel(tc, emb, pe, ln_w, ln_b, offs, out):
+    nc = tc.nc
+    with (
+        tc.tile_pool(name="held", bufs=1) as held,
+        tc.psum_pool(name="psum", bufs=1) as psum,
+    ):
+        offsets = held.tile([C, N // 16], U16, name="offsets")
+        nc.sync.dma_start(offsets[:], offs)
+        table = held.tile([C, S], F32, name="table")
+        nc.sync.dma_start(table[:], emb)
+        place = held.tile([C, N], F32, name="place")
+        nc.scalar.dma_start(place[:], pe)
+        gain = held.tile([C, 1], F32, name="gain")
+        nc.gpsimd.dma_start(gain[:], ln_w)
+        shift = held.tile([C, 1], F32, name="shift")
+        nc.gpsimd.dma_start(shift[:], ln_b)
+
+        centre = held.tile([C, C], F32, name="centre")
+        nc.gpsimd.memset(centre[:], -1.0 / C)
+        nc.gpsimd.affine_select(
+            out=centre[:],
+            in_=centre[:],
+            compare_op=ALU.not_equal,
+            fill=1.0 - 1.0 / C,
+            base=0,
+            pattern=[[-1, C]],
+            channel_multiplier=1,
+        )
+        average = held.tile([C, C], F32, name="average")
+        nc.vector.memset(average[:], 1.0 / C)
+        eps = held.tile([C, 1], F32, name="eps")
+        nc.vector.memset(eps[:], EPS)
+
+        x = held.tile([C, N], F32, name="x")
+        nc.vector.tensor_tensor(x[:], table[:].indirect(offsets[:]), place[:], ALU.add)
+        nc.sync.dma_start(out[0:C, :], x[:])
+
+        centred = psum.tile([C, N], F32, name="centred")
+        nc.tensor.matmul(centred[:], centre[:], x[:], start=True, stop=True)
+        squares = held.tile([C, N], F32, name="squares")
+        nc.scalar.activation(squares[:], centred[:], ACT.Square)
+        variance = psum.tile([C, N], F32, name="variance")
+        nc.tensor.matmul(variance[:], average[:], squares[:], start=True, stop=True)
+
+        spread = held.tile([C, N], F32, name="spread")
+        nc.scalar.activation(spread[:], variance[:], ACT.Sqrt, bias=eps[:])
+        inverse = held.tile([C, N], F32, name="inverse")
+        nc.vector.reciprocal(inverse[:], spread[:])
+
+        normed = held.tile([C, N], F32, name="normed")
+        nc.vector.tensor_tensor(normed[:], centred[:], inverse[:], ALU.mult)
+        h = held.tile([C, N], F32, name="h")
+        nc.vector.tensor_scalar(h[:], normed[:], gain[:], shift[:], ALU.mult, ALU.add)
+        nc.sync.dma_start(out[C : 2 * C, :], h[:])

@@ -23,9 +23,9 @@ def tile_transformernet_kernel(tc, emb, pe, ln_w, ln_b, offs, out):
         place = held.tile([C, N], F32, name="place")
         nc.scalar.dma_start(place[:], pe)
         gain = held.tile([C, 1], F32, name="gain")
-        nc.gpsimd.dma_start(gain[:], ln_w)
+        nc.scalar.dma_start(gain[:], ln_w)
         shift = held.tile([C, 1], F32, name="shift")
-        nc.gpsimd.dma_start(shift[:], ln_b)
+        nc.scalar.dma_start(shift[:], ln_b)
 
         centre = held.tile([C, C], F32, name="centre")
         nc.gpsimd.memset(centre[:], -1.0 / C)
@@ -42,6 +42,8 @@ def tile_transformernet_kernel(tc, emb, pe, ln_w, ln_b, offs, out):
         nc.vector.memset(average[:], 1.0 / C)
         eps = held.tile([C, 1], F32, name="eps")
         nc.vector.memset(eps[:], EPS)
+        first_use = held.tile([C, 1], F32, name="first_use")
+        nc.scalar.activation(first_use[:], eps[:], ACT.Abs_reciprocal_sqrt)
 
         x = held.tile([C, N], F32, name="x")
         nc.vector.tensor_tensor(x[:], table[:].indirect(offsets[:]), place[:], ALU.add)
@@ -54,10 +56,8 @@ def tile_transformernet_kernel(tc, emb, pe, ln_w, ln_b, offs, out):
         variance = psum.tile([C, N], F32, name="variance")
         nc.tensor.matmul(variance[:], average[:], squares[:], start=True, stop=True)
 
-        spread = held.tile([C, N], F32, name="spread")
-        nc.scalar.activation(spread[:], variance[:], ACT.Sqrt, bias=eps[:])
         inverse = held.tile([C, N], F32, name="inverse")
-        nc.vector.reciprocal(inverse[:], spread[:])
+        nc.scalar.activation(inverse[:], variance[:], ACT.Abs_reciprocal_sqrt, bias=eps[:])
 
         normed = held.tile([C, N], F32, name="normed")
         nc.vector.tensor_tensor(normed[:], centred[:], inverse[:], ALU.mult)

@@ -7,6 +7,8 @@ ACT = mybir.ActivationFunctionType
 
 C, S, N = 128, 512, 256
 EPS = 1e-6
+PIECES = 2
+W = N // PIECES
 FLOPS = 2 * 2 * C * C * N
 
 
@@ -45,22 +47,34 @@ def tile_transformernet_kernel(tc, emb, pe, ln_w, ln_b, offs, out):
         first_use = held.tile([C, 1], F32, name="first_use")
         nc.scalar.activation(first_use[:], eps[:], ACT.Abs_reciprocal_sqrt)
 
-        x = held.tile([C, N], F32, name="x")
-        nc.vector.tensor_tensor(x[:], table[:].indirect(offsets[:]), place[:], ALU.add)
-        nc.sync.dma_start(out[0:C, :], x[:])
+        pieces = range(PIECES)
+        x = [held.tile([C, W], F32, name=f"x{p}") for p in pieces]
+        centred = [psum.tile([C, W], F32, name=f"centred{p}") for p in pieces]
+        squares = [held.tile([C, W], F32, name=f"squares{p}") for p in pieces]
+        variance = [psum.tile([C, W], F32, name=f"variance{p}") for p in pieces]
+        inverse = [held.tile([C, W], F32, name=f"inverse{p}") for p in pieces]
+        normed = [held.tile([C, W], F32, name=f"normed{p}") for p in pieces]
+        h = [held.tile([C, W], F32, name=f"h{p}") for p in pieces]
 
-        centred = psum.tile([C, N], F32, name="centred")
-        nc.tensor.matmul(centred[:], centre[:], x[:], start=True, stop=True)
-        squares = held.tile([C, N], F32, name="squares")
-        nc.scalar.activation(squares[:], centred[:], ACT.Square)
-        variance = psum.tile([C, N], F32, name="variance")
-        nc.tensor.matmul(variance[:], average[:], squares[:], start=True, stop=True)
+        for p in pieces:
+            nc.vector.tensor_tensor(
+                x[p][:],
+                table[:].indirect(offsets[:, p * W // 16 : (p + 1) * W // 16]),
+                place[:, p * W : (p + 1) * W],
+                ALU.add,
+            )
+            nc.sync.dma_start(out[0:C, p * W : (p + 1) * W], x[p][:])
 
-        inverse = held.tile([C, N], F32, name="inverse")
-        nc.scalar.activation(inverse[:], variance[:], ACT.Abs_reciprocal_sqrt, bias=eps[:])
+        for p in pieces:
+            nc.tensor.matmul(centred[p][:], centre[:], x[p][:], start=True, stop=True)
+        for p in pieces:
+            nc.scalar.activation(squares[p][:], centred[p][:], ACT.Square)
+        for p in pieces:
+            nc.tensor.matmul(variance[p][:], average[:], squares[p][:], start=True, stop=True)
+        for p in pieces:
+            nc.scalar.activation(inverse[p][:], variance[p][:], ACT.Abs_reciprocal_sqrt, bias=eps[:])
 
-        normed = held.tile([C, N], F32, name="normed")
-        nc.vector.tensor_tensor(normed[:], centred[:], inverse[:], ALU.mult)
-        h = held.tile([C, N], F32, name="h")
-        nc.vector.tensor_scalar(h[:], normed[:], gain[:], shift[:], ALU.mult, ALU.add)
-        nc.sync.dma_start(out[C : 2 * C, :], h[:])
+        for p in pieces:
+            nc.vector.tensor_tensor(normed[p][:], centred[p][:], inverse[p][:], ALU.mult)
+            nc.vector.tensor_scalar(h[p][:], normed[p][:], gain[:], shift[:], ALU.mult, ALU.add)
+            nc.sync.dma_start(out[C : 2 * C, p * W : (p + 1) * W], h[p][:])

@@ -9,6 +9,7 @@ C, S, N = 128, 512, 256
 EPS = 1e-6
 PIECES = 2
 W = N // PIECES
+WARMING = 5
 FLOPS = 2 * 2 * C * C * N
 
 
@@ -46,6 +47,9 @@ def tile_transformernet_kernel(tc, emb, pe, ln_w, ln_b, offs, out):
         nc.vector.memset(eps[:], EPS)
         first_use = held.tile([C, 1], F32, name="first_use")
         nc.scalar.activation(first_use[:], eps[:], ACT.Abs_reciprocal_sqrt)
+        unread = psum.tile([C, C], F32, name="unread")
+        for _ in range(WARMING):
+            nc.tensor.matmul(unread[:], average[:], average[:], start=True, stop=True)
 
         pieces = range(PIECES)
         x = [held.tile([C, W], F32, name=f"x{p}") for p in pieces]

@@ -10,6 +10,7 @@ EPS = 1e-6
 PIECES = 2
 W = N // PIECES
 WARMING = 5
+HUGE = 2.0**96
 FLOPS = 2 * 2 * C * C * N
 
 
@@ -19,10 +20,10 @@ def tile_transformernet_kernel(tc, emb, pe, ln_w, ln_b, offs, out):
         tc.tile_pool(name="held", bufs=1) as held,
         tc.psum_pool(name="psum", bufs=1) as psum,
     ):
-        offsets = held.tile([C, N // 16], U16, name="offsets")
-        nc.sync.dma_start(offsets[:], offs)
         table = held.tile([C, S], F32, name="table")
         nc.sync.dma_start(table[:], emb)
+        offsets = held.tile([C, N // 16], U16, name="offsets")
+        nc.sync.dma_start(offsets[:], offs)
         place = held.tile([C, N], F32, name="place")
         nc.scalar.dma_start(place[:], pe)
         gain = held.tile([C, 1], F32, name="gain")
@@ -41,23 +42,33 @@ def tile_transformernet_kernel(tc, emb, pe, ln_w, ln_b, offs, out):
             pattern=[[-1, C]],
             channel_multiplier=1,
         )
-        average = held.tile([C, C], F32, name="average")
-        nc.vector.memset(average[:], 1.0 / C)
-        eps = held.tile([C, 1], F32, name="eps")
-        nc.vector.memset(eps[:], EPS)
+        floor = held.tile([W, W], F32, name="floor")
+        nc.gpsimd.memset(floor[:], HUGE)
+        nc.gpsimd.affine_select(
+            out=floor[:],
+            in_=floor[:],
+            compare_op=ALU.not_equal,
+            fill=EPS,
+            base=0,
+            pattern=[[-1, W]],
+            channel_multiplier=1,
+        )
+        ones = held.tile([C, C], F32, name="ones")
+        nc.vector.memset(ones[:], 1.0)
         first_use = held.tile([C, 1], F32, name="first_use")
-        nc.scalar.activation(first_use[:], eps[:], ACT.Abs_reciprocal_sqrt)
+        nc.scalar.activation(first_use[:], ones[:, 0:1], ACT.Abs_reciprocal_sqrt)
         unread = psum.tile([C, C], F32, name="unread")
         for _ in range(WARMING):
-            nc.tensor.matmul(unread[:], average[:], average[:], start=True, stop=True)
+            nc.tensor.matmul(unread[:], ones[:], ones[:], start=True, stop=True)
 
         pieces = range(PIECES)
         x = [held.tile([C, W], F32, name=f"x{p}") for p in pieces]
-        centred = [psum.tile([C, W], F32, name=f"centred{p}") for p in pieces]
-        squares = [held.tile([C, W], F32, name=f"squares{p}") for p in pieces]
-        variance = [psum.tile([C, W], F32, name=f"variance{p}") for p in pieces]
-        inverse = [held.tile([C, W], F32, name=f"inverse{p}") for p in pieces]
-        normed = [held.tile([C, W], F32, name=f"normed{p}") for p in pieces]
+        turned = [psum.tile([W, C], F32, name=f"turned{p}") for p in pieces]
+        weights = [held.tile([W, C], F32, name=f"weights{p}") for p in pieces]
+        squares = [held.tile([W, C], F32, name=f"squares{p}") for p in pieces]
+        variance = [held.tile([W, 1], F32, name=f"variance{p}") for p in pieces]
+        scaling = [held.tile([W, W], F32, name=f"scaling{p}") for p in pieces]
+        normed = [psum.tile([C, W], F32, name=f"normed{p}") for p in pieces]
         h = [held.tile([C, W], F32, name=f"h{p}") for p in pieces]
 
         for p in pieces:
@@ -70,15 +81,16 @@ def tile_transformernet_kernel(tc, emb, pe, ln_w, ln_b, offs, out):
             nc.sync.dma_start(out[0:C, p * W : (p + 1) * W], x[p][:])
 
         for p in pieces:
-            nc.tensor.matmul(centred[p][:], centre[:], x[p][:], start=True, stop=True)
+            nc.tensor.matmul(turned[p][:], x[p][:], centre[:], start=True, stop=True)
         for p in pieces:
-            nc.scalar.activation(squares[p][:], centred[p][:], ACT.Square)
+            nc.scalar.activation(
+                squares[p][:], turned[p][:], ACT.Square, scale=C**-0.5, accum_out=variance[p][:]
+            )
+            nc.vector.tensor_copy(weights[p][:], turned[p][:])
+            nc.scalar.activation(
+                scaling[p][:], floor[:], ACT.Abs_reciprocal_sqrt, bias=variance[p][:]
+            )
         for p in pieces:
-            nc.tensor.matmul(variance[p][:], average[:], squares[p][:], start=True, stop=True)
-        for p in pieces:
-            nc.scalar.activation(inverse[p][:], variance[p][:], ACT.Abs_reciprocal_sqrt, bias=eps[:])
-
-        for p in pieces:
-            nc.vector.tensor_tensor(normed[p][:], centred[p][:], inverse[p][:], ALU.mult)
+            nc.tensor.matmul(normed[p][:], weights[p][:], scaling[p][:], start=True, stop=True)
             nc.vector.tensor_scalar(h[p][:], normed[p][:], gain[:], shift[:], ALU.mult, ALU.add)
             nc.sync.dma_start(out[C : 2 * C, p * W : (p + 1) * W], h[p][:])

@@ -1,4 +1,5 @@
 import concourse.mybir as mybir
+from concourse.masks import make_identity
 
 F32 = mybir.dt.float32
 U16 = mybir.dt.uint16
@@ -10,8 +11,7 @@ EPS = 1e-6
 PIECES = 2
 W = N // PIECES
 WARMING = 5
-HUGE = 2.0**96
-FLOPS = 2 * 2 * C * C * N
+FLOPS = 2 * C * C * N
 
 
 def tile_transformernet_kernel(tc, emb, pe, ln_w, ln_b, offs, out):
@@ -42,17 +42,10 @@ def tile_transformernet_kernel(tc, emb, pe, ln_w, ln_b, offs, out):
             pattern=[[-1, C]],
             channel_multiplier=1,
         )
-        floor = held.tile([W, W], F32, name="floor")
-        nc.gpsimd.memset(floor[:], HUGE)
-        nc.gpsimd.affine_select(
-            out=floor[:],
-            in_=floor[:],
-            compare_op=ALU.not_equal,
-            fill=EPS,
-            base=0,
-            pattern=[[-1, W]],
-            channel_multiplier=1,
-        )
+        identity = held.tile([W, W], F32, name="identity")
+        make_identity(nc, identity[:])
+        eps = held.tile([W, 1], F32, name="eps")
+        nc.vector.memset(eps[:], EPS)
         ones = held.tile([C, C], F32, name="ones")
         nc.vector.memset(ones[:], 1.0)
         first_use = held.tile([C, 1], F32, name="first_use")
@@ -64,10 +57,10 @@ def tile_transformernet_kernel(tc, emb, pe, ln_w, ln_b, offs, out):
         pieces = range(PIECES)
         x = [held.tile([C, W], F32, name=f"x{p}") for p in pieces]
         turned = [psum.tile([W, C], F32, name=f"turned{p}") for p in pieces]
-        weights = [held.tile([W, C], F32, name=f"weights{p}") for p in pieces]
+        scaled = [held.tile([W, C], F32, name=f"scaled{p}") for p in pieces]
         squares = [held.tile([W, C], F32, name=f"squares{p}") for p in pieces]
         variance = [held.tile([W, 1], F32, name=f"variance{p}") for p in pieces]
-        scaling = [held.tile([W, W], F32, name=f"scaling{p}") for p in pieces]
+        inverse = [held.tile([W, 1], F32, name=f"inverse{p}") for p in pieces]
         normed = [psum.tile([C, W], F32, name=f"normed{p}") for p in pieces]
         h = [held.tile([C, W], F32, name=f"h{p}") for p in pieces]
 
@@ -86,11 +79,11 @@ def tile_transformernet_kernel(tc, emb, pe, ln_w, ln_b, offs, out):
             nc.scalar.activation(
                 squares[p][:], turned[p][:], ACT.Square, scale=C**-0.5, accum_out=variance[p][:]
             )
-            nc.vector.tensor_copy(weights[p][:], turned[p][:])
             nc.scalar.activation(
-                scaling[p][:], floor[:], ACT.Abs_reciprocal_sqrt, bias=variance[p][:]
+                inverse[p][:], variance[p][:], ACT.Abs_reciprocal_sqrt, bias=eps[:]
             )
+            nc.vector.tensor_scalar_mul(scaled[p][:], turned[p][:], inverse[p][:])
         for p in pieces:
-            nc.tensor.matmul(normed[p][:], weights[p][:], scaling[p][:], start=True, stop=True)
+            nc.tensor.transpose(normed[p][:], scaled[p][:], identity[:])
             nc.vector.tensor_scalar(h[p][:], normed[p][:], gain[:], shift[:], ALU.mult, ALU.add)
             nc.sync.dma_start(out[C : 2 * C, p * W : (p + 1) * W], h[p][:])

@@ -21,15 +21,15 @@ def tile_transformernet_kernel(tc, emb, pe, ln_w, ln_b, offs, out):
         tc.psum_pool(name="psum", bufs=1) as psum,
     ):
         table = held.tile([C, S], F32, name="table")
-        nc.sync.dma_start(table[:], emb)
+        nc.scalar.dma_start(table[:], emb)
+        place = held.tile([C, N], F32, name="place")
+        nc.sync.dma_start(place[:], pe)
         offsets = held.tile([C, N // 16], U16, name="offsets")
         nc.sync.dma_start(offsets[:], offs)
-        place = held.tile([C, N], F32, name="place")
-        nc.scalar.dma_start(place[:], pe)
         gain = held.tile([C, 1], F32, name="gain")
-        nc.scalar.dma_start(gain[:], ln_w)
+        nc.sync.dma_start(gain[:], ln_w)
         shift = held.tile([C, 1], F32, name="shift")
-        nc.scalar.dma_start(shift[:], ln_b)
+        nc.sync.dma_start(shift[:], ln_b)
 
         centre = held.tile([C, C], F32, name="centre")
         nc.gpsimd.memset(centre[:], -1.0 / C)

import concourse.mybir as mybir
from concourse.masks import make_identity

F32 = mybir.dt.float32
U16 = mybir.dt.uint16
ALU = mybir.AluOpType
ACT = mybir.ActivationFunctionType

C, S, N = 128, 512, 256
EPS = 1e-6
PIECES = 2
W = N // PIECES
WARMING = 5
FLOPS = 2 * C * C * N


def tile_transformernet_kernel(tc, emb, pe, ln_w, ln_b, offs, out):
    nc = tc.nc
    with (
        tc.tile_pool(name="held", bufs=1) as held,
        tc.psum_pool(name="psum", bufs=1) as psum,
    ):
        table = held.tile([C, S], F32, name="table")
        nc.scalar.dma_start(table[:], emb)
        place = held.tile([C, N], F32, name="place")
        nc.sync.dma_start(place[:], pe)
        offsets = held.tile([C, N // 16], U16, name="offsets")
        nc.sync.dma_start(offsets[:], offs)
        gain = held.tile([C, 1], F32, name="gain")
        nc.sync.dma_start(gain[:], ln_w)
        shift = held.tile([C, 1], F32, name="shift")
        nc.sync.dma_start(shift[:], ln_b)

        centre = held.tile([C, C], F32, name="centre")
        nc.gpsimd.memset(centre[:], -1.0 / C)
        nc.gpsimd.affine_select(
            out=centre[:],
            in_=centre[:],
            compare_op=ALU.not_equal,
            fill=1.0 - 1.0 / C,
            base=0,
            pattern=[[-1, C]],
            channel_multiplier=1,
        )
        identity = held.tile([W, W], F32, name="identity")
        make_identity(nc, identity[:])
        eps = held.tile([W, 1], F32, name="eps")
        nc.vector.memset(eps[:], EPS)
        ones = held.tile([C, C], F32, name="ones")
        nc.vector.memset(ones[:], 1.0)
        first_use = held.tile([C, 1], F32, name="first_use")
        nc.scalar.activation(first_use[:], ones[:, 0:1], ACT.Abs_reciprocal_sqrt)
        unread = psum.tile([C, C], F32, name="unread")
        for _ in range(WARMING):
            nc.tensor.matmul(unread[:], ones[:], ones[:], start=True, stop=True)

        pieces = range(PIECES)
        x = [held.tile([C, W], F32, name=f"x{p}") for p in pieces]
        turned = [psum.tile([W, C], F32, name=f"turned{p}") for p in pieces]
        scaled = [held.tile([W, C], F32, name=f"scaled{p}") for p in pieces]
        squares = [held.tile([W, C], F32, name=f"squares{p}") for p in pieces]
        variance = [held.tile([W, 1], F32, name=f"variance{p}") for p in pieces]
        inverse = [held.tile([W, 1], F32, name=f"inverse{p}") for p in pieces]
        normed = [psum.tile([C, W], F32, name=f"normed{p}") for p in pieces]
        h = [held.tile([C, W], F32, name=f"h{p}") for p in pieces]

        for p in pieces:
            nc.vector.tensor_tensor(
                x[p][:],
                table[:].indirect(offsets[:, p * W // 16 : (p + 1) * W // 16]),
                place[:, p * W : (p + 1) * W],
                ALU.add,
            )
            nc.sync.dma_start(out[0:C, p * W : (p + 1) * W], x[p][:])

        for p in pieces:
            nc.tensor.matmul(turned[p][:], x[p][:], centre[:], start=True, stop=True)
        for p in pieces:
            nc.scalar.activation(
                squares[p][:], turned[p][:], ACT.Square, scale=C**-0.5, accum_out=variance[p][:]
            )
            nc.scalar.activation(
                inverse[p][:], variance[p][:], ACT.Abs_reciprocal_sqrt, bias=eps[:]
            )
            nc.vector.tensor_scalar_mul(scaled[p][:], turned[p][:], inverse[p][:])
        for p in pieces:
            nc.tensor.transpose(normed[p][:], scaled[p][:], identity[:])
            nc.vector.tensor_scalar(h[p][:], normed[p][:], gain[:], shift[:], ALU.mult, ALU.add)
            nc.sync.dma_start(out[C : 2 * C, p * W : (p + 1) * W], h[p][:])
